import numpy as np
import ml_dtypes


def mxq(x, axis, fmt="e4m3"):
    dtype, down = {"e4m3": (ml_dtypes.float8_e4m3fn, 7), "e5m2": (ml_dtypes.float8_e5m2, 14)}[fmt]
    v = np.moveaxis(np.asarray(x, np.float32).astype(ml_dtypes.bfloat16).astype(np.float64), axis, -1)
    blocks = v.reshape(v.shape[:-1] + (-1, 32))
    amax = np.abs(blocks).max(-1, keepdims=True)
    byte = np.maximum(np.where(amax > 0, np.frexp(amax)[1] - 1 + 127, 0) - down, 1)
    scale = np.exp2(byte - 127.0)
    codes = (blocks / scale).astype(np.float32).astype(dtype).astype(np.float64)
    return np.moveaxis((codes * scale).reshape(v.shape), -1, axis)


WIDE = False


def mx_kscale(k):
    if not WIDE:
        return np.ones(k)
    levels = np.array([10, -10, 5, -5, 0])
    if k % 512:
        return np.exp2(np.random.permutation(np.resize(levels, k // 32))).repeat(32)
    a = np.empty((k // 512, 16))
    for p in range(k // 512):
        a[p, :8] = np.random.permutation(np.resize(levels, 8))
        for g in range(8):
            far = levels[np.abs(levels - a[p, g]) >= 10]
            a[p, g + 8] = far[np.random.randint(len(far))]
    return np.exp2(a.ravel()).repeat(32)


BF16 = ml_dtypes.bfloat16


def bf(x):
    return np.asarray(x, np.float32).astype(BF16)


def f64(x):
    return np.asarray(x).astype(np.float64)


E2M1 = np.array([0.0, 0.5, 1.0, 1.5, 2.0, 3.0, 4.0, 6.0, -0.0, -0.5, -1.0, -1.5, -2.0, -3.0, -4.0, -6.0])


def pack_weight(w, fmt):
    k, n = w.shape
    w = f64(bf(w)).reshape(k // 32, 32, n)
    amax = np.abs(w).max(1)
    if fmt == "e4m3":
        byte = np.frexp(amax)[1] - 1 + 127 - 7
    else:
        mant, ex = np.frexp(amax / 6.0)
        byte = np.where(mant > 0.5, ex, ex - 1) + 127
    byte = np.clip(np.where(amax > 0, byte, 1), 1, 254)
    scaled = (w * np.exp2(127.0 - byte)[:, None, :]).reshape(k, n).astype(np.float32)
    by_word = np.ascontiguousarray(scaled.reshape(k // 512, 128, 4, n).transpose(0, 1, 3, 2))
    if fmt == "e4m3":
        words = by_word.astype(ml_dtypes.float8_e4m3fn).view(np.uint8)
    else:
        c = by_word.astype(ml_dtypes.float4_e2m1fn).view(np.uint8) & 0xF
        words = c[..., 0::2] | (c[..., 1::2] << 4)
    return np.ascontiguousarray(words), np.ascontiguousarray(byte.astype(np.uint8).reshape(k // 512, 16, n))


def unpack_weight(words, scales, fmt):
    g, p, n, _ = words.shape
    if fmt == "e4m3":
        vals = np.ascontiguousarray(words).view(ml_dtypes.float8_e4m3fn).astype(np.float64)
    else:
        nib = np.empty((g, p, n, 4), np.uint8)
        nib[..., 0::2] = words & 0xF
        nib[..., 1::2] = words >> 4
        vals = E2M1[nib]
    vals = vals * np.repeat(np.exp2(scales.astype(np.float64) - 127.0), 8, axis=1)[..., None]
    return vals.transpose(0, 1, 3, 2).reshape(g * 512, n)
def pack4(w):
    words, scales = pack_weight(w, "e2m1")
    return words.reshape(words.shape[0], 128, -1), scales


def unpack4(words, scales):
    return unpack_weight(words.reshape(words.shape[0], 128, -1, 2), scales, "e2m1")


B, S, D, H, F = 4, 256, 1024, 16, 4096
EPS = 1e-5
NTERMS = 120


def layernorm(v, gamma, beta):
    mu = v.mean(-1, keepdims=True)
    var = np.square(v - mu).mean(-1, keepdims=True)
    return (v - mu) / np.sqrt(var + EPS) * gamma + beta


def erf(z):
    z = np.clip(z, -6.0, 6.0)
    zz = 2.0 * z * z
    term = z.copy()
    tot = z.copy()
    for n in range(1, NTERMS):
        term *= zz
        term /= 2.0 * n + 1.0
        tot += term
    return 2.0 / np.sqrt(np.pi) * np.exp(-z * z) * tot


def gelu(v):
    return 0.5 * v * (1.0 + erf(v / np.sqrt(2.0)))


def draw0():
    s, t = mx_kscale(D), mx_kscale(D)
    attn_out = bf(0.25 * np.random.standard_normal((B, S, D)) * s)
    x = bf(np.random.standard_normal((B, S, D)) * (0.5 + np.random.random((B, S, 1))) + 0.5 * np.random.standard_normal((B, S, 1)))
    w_proj_words, w_proj_scales = pack4(2.0 * np.random.standard_normal((D, D)) / np.sqrt(D) / s[:, None])
    b_proj = bf(0.1 * np.random.standard_normal(D))
    g2 = bf((1.0 + 0.1 * np.random.standard_normal(D)) * t)
    beta2 = bf(0.1 * np.random.standard_normal(D) * t)
    w_fc1_words, w_fc1_scales = pack4(np.random.standard_normal((D, F)) / np.sqrt(D) / t[:, None])
    b_fc1 = bf(0.1 * np.random.standard_normal(F))
    return {"attn_out": attn_out,
            "x": x,
            "w_proj_words": w_proj_words,
            "w_proj_scales": w_proj_scales,
            "b_proj": b_proj,
            "g2": g2,
            "beta2": beta2,
            "w_fc1_words": w_fc1_words,
            "w_fc1_scales": w_fc1_scales,
            "b_fc1": b_fc1}


def core(attn_out, x, w_proj_words, w_proj_scales, b_proj, g2, beta2, w_fc1_words, w_fc1_scales, b_fc1):
    x_mid = f64(x) + ((mxq(f64(attn_out), 2, "e4m3") @ unpack4(w_proj_words, w_proj_scales)) + f64(b_proj))
    h = layernorm(x_mid, f64(g2), f64(beta2))
    hid = gelu((mxq(h, 2, "e4m3") @ unpack4(w_fc1_words, w_fc1_scales)) + f64(b_fc1))
    return x_mid, hid


def e4m3fn_bytes(y):
    return np.clip(np.asarray(y, np.float64), -448.0, 448.0).astype(np.float32).astype(ml_dtypes.float8_e4m3fn).view(np.uint8)


def e4m3fn_values(b):
    return np.asarray(b, np.uint8).view(ml_dtypes.float8_e4m3fn).astype(np.float64)


def setup_inputs():
    d = draw0()
    x0 = np.asarray(d['attn_out']).astype(np.float64)
    s = (np.max(np.abs(x0), axis=(0, 1), keepdims=True) / 448.0).astype(np.float32)
    out = {}
    for k, v in d.items():
        if k == 'attn_out':
            out['attn_out_bytes'] = e4m3fn_bytes(x0 / s.astype(np.float64))
            out['attn_out_scale'] = s
        else:
            out[k] = v
    return out


def reference(attn_out_bytes, attn_out_scale, x, w_proj_words, w_proj_scales, b_proj, g2, beta2, w_fc1_words, w_fc1_scales, b_fc1):
    return core(e4m3fn_values(attn_out_bytes) * attn_out_scale.astype(np.float64), x, w_proj_words, w_proj_scales, b_proj, g2, beta2, w_fc1_words, w_fc1_scales, b_fc1)

@@ -1,0 +1,349 @@
+from contextlib import ExitStack
+
+import concourse.mybir as mybir
+from concourse.masks import make_identity
+
+P = 128
+TILES = 8
+D = 1024
+F = 4096
+GROUPS = 2
+PACK = 4
+BLOCK = 512
+EPS = 1e-5
+AHEAD = 2.5
+CAP = 8
+V_PRE = 1
+PROD_SG = ()
+WEAVE_G = ()
+WEAVE_S = ()
+NORM_G = ()
+GAIN_V = ()
+LAY_V = ()
+G_CUT = 1
+OFF = {
+    "widen": (-25.5, 2.5),
+    "turn_attn": (-23, 0),
+    "lay_attn": (-22, 0),
+    "quant_attn": (-20.5, 0),
+    "pre_add": (-22.5, 0),
+    "project": (-19.5, 0),
+    "mid": (-17, 0),
+    "mean": (-16.9, 0),
+    "spread": (-16, 0),
+    "rstd": (-15.5, 0),
+    "norm": (-14, 0),
+    "turn_norm0": (-13, 0),
+    "turn_norm1": (-13.5, 0),
+    "gain0": (-13, 0),
+    "gain1": (-11.5, 0),
+    "weave0": (-9, 0),
+    "weave1": (-8, 0),
+    "quant_norm": (-4.9, 0),
+}
+
+FLOPS = 2 * TILES * P * D * (D + F)
+
+F32 = mybir.dt.float32
+BF16 = mybir.dt.bfloat16
+I32 = mybir.dt.int32
+U32 = mybir.dt.uint32
+U8 = mybir.dt.uint8
+F8 = mybir.dt.float8_e4m3fn
+FP8X4 = mybir.dt.float8_e4m3fn_x4
+FP4X4 = mybir.dt.float4_e2m1fn_x4
+
+ADD = mybir.AluOpType.add
+MULT = mybir.AluOpType.mult
+POW = mybir.AluOpType.pow
+IDENTITY = mybir.ActivationFunctionType.Identity
+SQUARE = mybir.ActivationFunctionType.Square
+GELU = mybir.ActivationFunctionType.Gelu
+
+
+def tile_flashinferblock_pb_w4_kernel(
+    tc, attn_out_bytes, attn_out_scale, x, w_proj_words, w_proj_scales, b_proj, g2, beta2,
+    w_fc1_words, w_fc1_scales, b_fc1, out_0, out_1,
+):
+    nc = tc.nc
+    with ExitStack() as ctx:
+        keep = ctx.enter_context(tc.tile_pool(name="keep", bufs=1))
+        work = ctx.enter_context(tc.tile_pool(name="work", bufs=2))
+        work3 = ctx.enter_context(tc.tile_pool(name="work3", bufs=3))
+        hids = ctx.enter_context(tc.tile_pool(name="hids", bufs=8))
+        ps_turn = ctx.enter_context(tc.psum_pool(name="ps_turn", bufs=3))
+        ps_proj = ctx.enter_context(tc.psum_pool(name="ps_proj", bufs=2))
+        ps_hid = ctx.enter_context(tc.psum_pool(name="ps_hid", bufs=3))
+
+        attn_hbm = attn_out_bytes.flatten_outer_dims().rearrange("(p i) d -> p i d", i=TILES)
+        x_hbm = x.flatten_outer_dims().rearrange("(p i) d -> p i d", i=TILES)
+        mid_hbm = out_0.flatten_outer_dims().rearrange("(p i) d -> p i d", i=TILES)
+        hid_hbm = out_1.flatten_outer_dims().rearrange("(p i) f -> p i f", i=TILES)
+
+        attn_codes = keep.tile([P, TILES, D], U8, name="attn_codes", align_bytes=64)
+        scale_all = keep.tile([P, D], F32, name="scale_all", align_bytes=64)
+        x_all = keep.tile([P, TILES, D], BF16, name="x_all", align_bytes=64)
+        bp_all = keep.tile([P, D], BF16, name="bp_all", align_bytes=64)
+        bf_all = keep.tile([P, F], BF16, name="bf_all", align_bytes=64)
+        wp = keep.tile([P, GROUPS, 2 * D], U8, name="wp", align_bytes=64)
+        wp_sc = keep.tile([P, GROUPS, D], U8, name="wp_sc", align_bytes=64)
+        wf = keep.tile([P, GROUPS, 2 * F], U8, name="wf", align_bytes=64)
+        wf_sc = keep.tile([P, GROUPS, F], U8, name="wf_sc", align_bytes=64)
+        g_raw = keep.tile([P, GROUPS, PACK], BF16, name="g_raw", align_bytes=64)
+        b_raw = keep.tile([P, GROUPS, PACK], BF16, name="b_raw", align_bytes=64)
+        g_col = keep.tile([P, GROUPS, PACK], F32, name="g_col", align_bytes=64)
+        b_col = keep.tile([P, GROUPS, PACK], F32, name="b_col", align_bytes=64)
+        ident = keep.tile([P, P], F32, name="ident", align_bytes=64)
+        half = keep.tile([P, 1], F32, name="half", align_bytes=64)
+        warm = keep.tile([P, 1], F32, name="warm", align_bytes=64)
+
+        nc.vector.memset(wp_sc[:].rearrange("p g n -> p (g n)").bitcast(I32), 0)
+        nc.vector.memset(wf_sc[:].rearrange("p g n -> p (g n)").bitcast(I32), 0)
+        nc.vector.memset(warm[:], 0.0)
+        nc.gpsimd.memset(half[:], -0.5)
+        make_identity(nc, ident[:])
+        nc.scalar.activation(out=warm[:], in_=warm[:], func=GELU)
+
+        def load_scales(tile, hbm):
+            for q in range(4):
+                nc.sync.dma_start(
+                    out=tile[32 * q : 32 * q + 4, :, :].bitcast(I32),
+                    in_=hbm[:, 4 * q : 4 * q + 4, :].rearrange("g q n -> q g n").bitcast(I32),
+                )
+
+        def load_attn(a, b):
+            nc.sync.dma_start(out=attn_codes[:, a:b, :], in_=attn_hbm[:, a:b, :])
+
+        def load_x(a, b):
+            nc.sync.dma_start(out=x_all[:, a:b, :], in_=x_hbm[:, a:b, :])
+
+        def load_wf(a, b):
+            nc.sync.dma_start(
+                out=wf[:, :, a:b].bitcast(I32),
+                in_=w_fc1_words[:, :, a:b].rearrange("g p b -> p g b").bitcast(I32),
+            )
+
+        nc.scalar.dma_start(out=scale_all[:], in_=attn_out_scale.rearrange("a b k -> (a b k)").partition_broadcast(P))
+        load_attn(0, 1)
+        load_x(0, 1)
+        nc.scalar.dma_start(out=bp_all[:], in_=b_proj.partition_broadcast(P))
+        nc.sync.dma_start(out=wp[:], in_=w_proj_words.rearrange("g p b -> p g b"))
+        load_scales(wp_sc, w_proj_scales)
+        load_attn(1, 4)
+        for raw, vec in ((g_raw, g2), (b_raw, beta2)):
+            nc.scalar.dma_start(out=raw[:], in_=vec.rearrange("(g p t) -> p g t", p=P, t=PACK))
+        load_x(1, 3)
+        load_scales(wf_sc, w_fc1_scales)
+        load_wf(0, F)
+        nc.scalar.dma_start(out=bf_all[:], in_=b_fc1.partition_broadcast(P))
+        load_attn(4, 8)
+        load_wf(F, 2 * F)
+        load_x(3, 8)
+
+        state = {}
+
+        def widen(i):
+            prod = keep.tile([P, D], BF16, name="prod%d" % i, align_bytes=64)
+            if i in PROD_SG:
+                wide = work.tile([P, D], BF16, name="wide", align_bytes=64)
+                nc.scalar.copy(out=wide[:], in_=attn_codes[:, i, :].bitcast(F8))
+                for c in range(G_CUT):
+                    cols = slice(D // G_CUT * c, D // G_CUT * (c + 1))
+                    nc.gpsimd.tensor_tensor(out=prod[:, cols], in0=wide[:, cols], in1=scale_all[:, cols], op=MULT)
+                state["prod", i] = prod
+                return
+            nc.vector.tensor_tensor(out=prod[:], in0=attn_codes[:, i, :].bitcast(F8), in1=scale_all[:], op=MULT)
+            state["prod", i] = prod
+
+        def turn_attn(i):
+            words = state["prod", i][:].bitcast(F32)
+            turned = ps_turn.tile([P, GROUPS, 2, P], F32, name="turned")
+            for g in range(GROUPS):
+                for u in range(2):
+                    nc.tensor.transpose(turned[:, g, u, :], words[:, 256 * g + u : 256 * (g + 1) : 2], ident[:])
+            state["turned", i] = turned
+
+        def lay_attn(i):
+            ag = work.tile([P, D], BF16, name="ag", align_bytes=64)
+            lay_copy = nc.vector.tensor_copy if i in LAY_V else nc.scalar.copy
+            lay_copy(
+                out=ag[:].bitcast(F32).rearrange("p (g r u) -> p g r u", g=GROUPS, u=2),
+                in_=state["turned", i][:].rearrange("p g u r -> p g r u"),
+            )
+            state["ag", i] = ag
+
+        def quant_attn(i):
+            aq = work3.tile([P, GROUPS * P], U32, name="aq", align_bytes=64)
+            asc = work3.tile([P, GROUPS * P], U8, name="asc", align_bytes=64)
+            nc.vector.quantize_mx(out=aq[:].bitcast(FP8X4), scales=asc[:], in_=state["ag", i][:])
+            state["aq", i] = (aq, asc)
+
+        def pre_add(i):
+            xb = work3.tile([P, D], F32, name="xb", align_bytes=64)
+            eng = nc.vector if i < V_PRE else nc.gpsimd
+            for c in range(1 if i < V_PRE else G_CUT):
+                cols = slice(0, D) if i < V_PRE else slice(D // G_CUT * c, D // G_CUT * (c + 1))
+                eng.tensor_tensor(out=xb[:, cols], in0=x_all[:, i, cols], in1=bp_all[:, cols], op=ADD)
+            state["xb", i] = xb
+
+        def project(i):
+            aq, asc = state["aq", i]
+            for n in range(2):
+                acc = ps_proj.tile([P, BLOCK], F32, name="acc")
+                for g in range(GROUPS):
+                    nc.tensor.matmul_mx(
+                        out=acc[:],
+                        lhsT=aq[:, P * g : P * (g + 1)].bitcast(FP8X4),
+                        lhsT_scale=asc[:, P * g : P * (g + 1)],
+                        rhs=wp[:, g, 2 * BLOCK * n : 2 * BLOCK * (n + 1)].bitcast(FP4X4),
+                        rhs_scale=wp_sc[:, g, BLOCK * n : BLOCK * (n + 1)],
+                        start=(g == 0),
+                        stop=(g == GROUPS - 1),
+                    )
+                state["acc", i, n] = acc
+
+        def mid(i):
+            xm = work3.tile([P, D], F32, name="xm", align_bytes=64)
+            sums = work3.tile([P, 2], F32, name="sums", align_bytes=64)
+            for n in range(2):
+                cols = slice(BLOCK * n, BLOCK * (n + 1))
+                nc.vector.scalar_tensor_tensor(
+                    out=xm[:, cols], in0=state["acc", i, n][:], scalar=1.0, in1=state["xb", i][:, cols],
+                    op0=MULT, op1=ADD, accum_out=sums[:, n : n + 1],
+                )
+            state["xm", i] = xm
+            state["sums", i] = sums
+            nc.sync.dma_start(out=mid_hbm[:, i, :], in_=xm[:])
+
+        def mean(i):
+            sums = state["sums", i]
+            nmu = work3.tile([P, 1], F32, name="nmu", align_bytes=64)
+            nc.gpsimd.tensor_scalar(out=nmu[:], in0=sums[:, 0:1], scalar1=sums[:, 1:2], scalar2=-1.0 / D, op0=ADD, op1=MULT)
+            state["xm", i] = (state["xm", i], nmu)
+
+        def spread(i):
+            if i == 0:
+                nc.gpsimd.tensor_copy(out=g_col[:], in_=g_raw[:])
+                nc.gpsimd.tensor_copy(out=b_col[:], in_=b_raw[:])
+            xm, nmu = state["xm", i]
+            junk = work.tile([P, D], BF16, name="junk", align_bytes=64)
+            ssq = work3.tile([P, 1], F32, name="ssq", align_bytes=64)
+            nc.scalar.activation(out=junk[:], in_=xm[:], func=SQUARE, bias=nmu[:], scale=1.0, accum_out=ssq[:])
+            state["ssq", i] = ssq
+
+        def rstd(i):
+            ssq = state["ssq", i]
+            var = work3.tile([P, 1], F32, name="var", align_bytes=64)
+            rs = work3.tile([P, 1], F32, name="rs", align_bytes=64)
+            nc.gpsimd.tensor_scalar(out=var[:], in0=ssq[:], scalar1=1.0 / D, scalar2=EPS, op0=MULT, op1=ADD)
+            nc.gpsimd.tensor_tensor(out=rs[:], in0=var[:], in1=half[:], op=POW)
+            state["rstd", i] = rs
+
+        def norm(i):
+            xm, nmu = state["xm", i]
+            xh = work.tile([P, D], F32, name="xh", align_bytes=64)
+            eng = nc.gpsimd if i in NORM_G else nc.vector
+            eng.tensor_scalar(
+                out=xh[:].rearrange("p (g t q) -> p g q t", g=GROUPS, t=PACK),
+                in0=xm[:].rearrange("p (g q t) -> p g q t", g=GROUPS, t=PACK),
+                scalar1=nmu[:], scalar2=state["rstd", i][:], op0=ADD, op1=MULT,
+            )
+            state["xh", i] = xh
+
+        def turn_norm(i, g):
+            xh = state["xh", i]
+            turned = ps_turn.tile([P, PACK, P], F32, name="turned")
+            for t in range(PACK):
+                j = PACK * g + t
+                nc.tensor.transpose(turned[:, t, :], xh[:, P * j : P * (j + 1)], ident[:])
+            state["hturned", i, g] = turned
+
+        def gain(i, g):
+            ht = work3.tile([P, PACK, P], BF16, name="ht", align_bytes=64)
+            for t in range(PACK):
+                if (i, g) in GAIN_V:
+                    nc.vector.tensor_scalar(
+                        out=ht[:, t, :], in0=state["hturned", i, g][:, t, :],
+                        scalar1=g_col[:, g, t : t + 1], scalar2=b_col[:, g, t : t + 1], op0=MULT, op1=ADD,
+                    )
+                    continue
+                nc.scalar.activation(
+                    out=ht[:, t, :], in_=state["hturned", i, g][:, t, :], func=IDENTITY,
+                    bias=b_col[:, g, t : t + 1], scale=g_col[:, g, t : t + 1],
+                )
+            state["ht", i, g] = ht
+
+        def weave(i, g):
+            if g == 0:
+                state["hg", i] = work.tile([P, GROUPS, BLOCK], BF16, name="hg", align_bytes=64)
+            state["woven", i, g] = True
+            dst = state["hg", i][:, g, :].rearrange("p (c i t) -> p c t i", i=4, t=PACK)
+            src = state["ht", i, g][:].rearrange("p t (c i) -> p c t i", i=4)
+            if i in WEAVE_G:
+                nc.gpsimd.tensor_scalar(out=dst, in0=src, scalar1=1.0, scalar2=0.0, op0=MULT, op1=ADD)
+            elif i in WEAVE_S:
+                nc.scalar.copy(out=dst, in_=src)
+            else:
+                nc.vector.tensor_copy(out=dst, in_=src)
+
+        def quant_norm(i):
+            assert state["woven", i, 0] and state["woven", i, 1]
+            hq = work.tile([P, GROUPS * P], U32, name="hq", align_bytes=64)
+            hsc = work.tile([P, GROUPS * P], U8, name="hsc", align_bytes=64)
+            nc.vector.quantize_mx(
+                out=hq[:].bitcast(FP8X4), scales=hsc[:], in_=state["hg", i][:].rearrange("p g c -> p (g c)")
+            )
+            state["hq", i] = (hq, hsc)
+
+        def expand(i, f):
+            hq, hsc = state["hq", i]
+            acc = ps_hid.tile([P, BLOCK], F32, name="hacc")
+            for g in range(GROUPS):
+                nc.tensor.matmul_mx(
+                    out=acc[:],
+                    lhsT=hq[:, P * g : P * (g + 1)].bitcast(FP8X4),
+                    lhsT_scale=hsc[:, P * g : P * (g + 1)],
+                    rhs=wf[:, g, 2 * BLOCK * f : 2 * BLOCK * (f + 1)].bitcast(FP4X4),
+                    rhs_scale=wf_sc[:, g, BLOCK * f : BLOCK * (f + 1)],
+                    start=(g == 0),
+                    stop=(g == GROUPS - 1),
+                )
+            state["hacc", i, f] = acc
+
+        def bias(i, f):
+            if f % 2 == 0:
+                state["hid", i, f // 2] = hids.tile([P, 2 * BLOCK], F32, name="hid", align_bytes=64)
+            hid = state["hid", i, f // 2]
+            o = BLOCK * (f % 2)
+            nc.vector.tensor_tensor(
+                out=hid[:, o : o + BLOCK], in0=state["hacc", i, f][:], in1=bf_all[:, BLOCK * f : BLOCK * (f + 1)], op=ADD
+            )
+
+        def act(i, h):
+            hid = state["hid", i, h]
+            parts = 2 if (i == TILES - 1 and h == 3) else 1
+            w = 2 * BLOCK // parts
+            for c in range(parts):
+                nc.scalar.activation(out=hid[:, w * c : w * (c + 1)], in_=hid[:, w * c : w * (c + 1)], func=GELU)
+                nc.sync.dma_start(out=hid_hbm[:, i, 2 * BLOCK * h + w * c : 2 * BLOCK * h + w * (c + 1)], in_=hid[:, w * c : w * (c + 1)])
+
+        stages = {
+            "widen": widen, "turn_attn": turn_attn, "lay_attn": lay_attn, "quant_attn": quant_attn, "pre_add": pre_add,
+            "project": project, "mid": mid, "mean": mean, "spread": spread, "rstd": rstd, "norm": norm,
+            "turn_norm0": lambda j: turn_norm(j, 0), "turn_norm1": lambda j: turn_norm(j, 1),
+            "gain0": lambda j: gain(j, 0), "gain1": lambda j: gain(j, 1),
+            "weave0": lambda j: weave(j, 0), "weave1": lambda j: weave(j, 1), "quant_norm": quant_norm,
+        }
+        events = []
+        for j in range(TILES):
+            for order, (name, (off, early)) in enumerate(OFF.items()):
+                events.append((8 * j + off - min(early * j, CAP), order + 100, stages[name], (j,)))
+            for f in range(8):
+                events.append((8 * j + f - AHEAD, 0, expand, (j, f)))
+                events.append((8 * j + f, 1, bias, (j, f)))
+                if f % 2 == 1:
+                    events.append((8 * j + f, 2, act, (j, f // 2)))
+        events.sort(key=lambda e: e[:2])
+        with tc.manual_schedule():
+            for e in events:
+                e[2](*e[3])

@@ -11,36 +11,48 @@ GROUPS = 2
 PACK = 4
 BLOCK = 512
 EPS = 1e-5
-AHEAD = 2.5
-CAP = 8
-V_PRE = 1
+V_PRE = 3
 PROD_SG = ()
 WEAVE_G = ()
 WEAVE_S = ()
 NORM_G = ()
 GAIN_V = ()
 LAY_V = ()
-G_CUT = 1
-OFF = {
-    "widen": (-25.5, 2.5),
-    "turn_attn": (-23, 0),
-    "lay_attn": (-22, 0),
-    "quant_attn": (-20.5, 0),
-    "pre_add": (-22.5, 0),
-    "project": (-19.5, 0),
-    "mid": (-17, 0),
-    "mean": (-16.9, 0),
-    "spread": (-16, 0),
-    "rstd": (-15.5, 0),
-    "norm": (-14, 0),
-    "turn_norm0": (-13, 0),
-    "turn_norm1": (-13.5, 0),
-    "gain0": (-13, 0),
-    "gain1": (-11.5, 0),
-    "weave0": (-9, 0),
-    "weave1": (-8, 0),
-    "quant_norm": (-4.9, 0),
-}
+G_CUT = 2
+NAMES = (
+    "widen turn_attn lay_attn quant_attn pre_add0 pre_add1 project0 project1 mid0 mid1 mean spread rstd norm turn_norm0 turn_norm1 "
+    "gain0 weave0 gain1 weave1 quant_norm "
+    "expand0 bias0 expand1 bias1 act0 expand2 bias2 expand3 bias3 act1 expand4 bias4 expand5 bias5 act2 expand6 bias6 expand7 bias7 act3"
+).split(" ")
+WEAVE_AT = 5
+HEAD = (
+    ("widen turn_attn lay_attn", 0),
+    ("widen turn_attn lay_attn", 1),
+    ("pre_add0", 0),
+    ("quant_attn project0 project1", 0),
+    ("pre_add1", 0),
+    ("mid0 mid1 mean spread", 0),
+    ("widen turn_attn lay_attn", 2),
+    ("quant_attn project0 project1", 1),
+    ("var rstd", 0),
+    ("pre_add0 pre_add1", 1),
+    ("norm turn_norm0 turn_norm1 gain0 gain1", 0),
+    ("mid0 mid1 mean spread", 1),
+    ("var rstd", 1),
+    ("quant_attn", 2),
+    ("weave0", 0),
+    ("pre_add0", 2),
+    ("weave1", 0),
+    ("pre_add1", 2),
+    ("quant_norm", 0),
+    ("project0 project1", 2),
+    ("widen turn_attn lay_attn", 3),
+    ("expand0 expand1", 0),
+)
+FRONT = {0: (2,), 1: (3,), 2: (4,), 3: (5,), 4: (6,), 5: (7,)}
+QUANT = {0: (3,), 1: (4,), 2: (5,), 3: (6,), 4: (7,)}
+WIDE = {0: (4,), 1: (5,), 2: (6,), 3: (7,)}
+PRE = {0: (3,), 1: (4,), 2: (5,), 3: (6,), 4: (7,)}
 
 FLOPS = 2 * TILES * P * D * (D + F)
 
@@ -57,6 +69,7 @@ ADD = mybir.AluOpType.add
 MULT = mybir.AluOpType.mult
 POW = mybir.AluOpType.pow
 IDENTITY = mybir.ActivationFunctionType.Identity
+COPY = mybir.ActivationFunctionType.Copy
 SQUARE = mybir.ActivationFunctionType.Square
 GELU = mybir.ActivationFunctionType.Gelu
 
@@ -69,7 +82,7 @@ def tile_flashinferblock_pb_w4_kernel(
     with ExitStack() as ctx:
         keep = ctx.enter_context(tc.tile_pool(name="keep", bufs=1))
         work = ctx.enter_context(tc.tile_pool(name="work", bufs=2))
-        work3 = ctx.enter_context(tc.tile_pool(name="work3", bufs=3))
+        work3 = ctx.enter_context(tc.tile_pool(name="work3", bufs=4))
         hids = ctx.enter_context(tc.tile_pool(name="hids", bufs=8))
         ps_turn = ctx.enter_context(tc.psum_pool(name="ps_turn", bufs=3))
         ps_proj = ctx.enter_context(tc.psum_pool(name="ps_proj", bufs=2))
@@ -125,19 +138,20 @@ def tile_flashinferblock_pb_w4_kernel(
 
         nc.scalar.dma_start(out=scale_all[:], in_=attn_out_scale.rearrange("a b k -> (a b k)").partition_broadcast(P))
         load_attn(0, 1)
-        load_x(0, 1)
-        nc.scalar.dma_start(out=bp_all[:], in_=b_proj.partition_broadcast(P))
-        nc.sync.dma_start(out=wp[:], in_=w_proj_words.rearrange("g p b -> p g b"))
+        load_attn(1, 2)
         load_scales(wp_sc, w_proj_scales)
-        load_attn(1, 4)
+        nc.sync.dma_start(out=wp[:], in_=w_proj_words.rearrange("g p b -> p g b"))
+        nc.scalar.dma_start(out=bp_all[:], in_=b_proj.partition_broadcast(P))
+        load_x(0, 1)
+        load_attn(2, 4)
+        load_x(1, 3)
         for raw, vec in ((g_raw, g2), (b_raw, beta2)):
             nc.scalar.dma_start(out=raw[:], in_=vec.rearrange("(g p t) -> p g t", p=P, t=PACK))
-        load_x(1, 3)
         load_scales(wf_sc, w_fc1_scales)
         load_wf(0, F)
         nc.scalar.dma_start(out=bf_all[:], in_=b_fc1.partition_broadcast(P))
-        load_attn(4, 8)
         load_wf(F, 2 * F)
+        load_attn(4, 8)
         load_x(3, 8)
 
         state = {}
@@ -178,65 +192,63 @@ def tile_flashinferblock_pb_w4_kernel(
             nc.vector.quantize_mx(out=aq[:].bitcast(FP8X4), scales=asc[:], in_=state["ag", i][:])
             state["aq", i] = (aq, asc)
 
-        def pre_add(i):
-            xb = work3.tile([P, D], F32, name="xb", align_bytes=64)
+        def pre_add(i, c):
+            if ("xb", i) not in state:
+                state["xb", i] = work3.tile([P, D], F32, name="xb", align_bytes=64)
+            xb = state["xb", i]
             eng = nc.vector if i < V_PRE else nc.gpsimd
-            for c in range(1 if i < V_PRE else G_CUT):
-                cols = slice(0, D) if i < V_PRE else slice(D // G_CUT * c, D // G_CUT * (c + 1))
-                eng.tensor_tensor(out=xb[:, cols], in0=x_all[:, i, cols], in1=bp_all[:, cols], op=ADD)
-            state["xb", i] = xb
+            cols = slice(BLOCK * c, BLOCK * (c + 1))
+            eng.tensor_tensor(out=xb[:, cols], in0=x_all[:, i, cols], in1=bp_all[:, cols], op=ADD)
 
-        def project(i):
+        def project(i, n):
             aq, asc = state["aq", i]
-            for n in range(2):
-                acc = ps_proj.tile([P, BLOCK], F32, name="acc")
-                for g in range(GROUPS):
-                    nc.tensor.matmul_mx(
-                        out=acc[:],
-                        lhsT=aq[:, P * g : P * (g + 1)].bitcast(FP8X4),
-                        lhsT_scale=asc[:, P * g : P * (g + 1)],
-                        rhs=wp[:, g, 2 * BLOCK * n : 2 * BLOCK * (n + 1)].bitcast(FP4X4),
-                        rhs_scale=wp_sc[:, g, BLOCK * n : BLOCK * (n + 1)],
-                        start=(g == 0),
-                        stop=(g == GROUPS - 1),
-                    )
-                state["acc", i, n] = acc
-
-        def mid(i):
-            xm = work3.tile([P, D], F32, name="xm", align_bytes=64)
-            sums = work3.tile([P, 2], F32, name="sums", align_bytes=64)
-            for n in range(2):
-                cols = slice(BLOCK * n, BLOCK * (n + 1))
-                nc.vector.scalar_tensor_tensor(
-                    out=xm[:, cols], in0=state["acc", i, n][:], scalar=1.0, in1=state["xb", i][:, cols],
-                    op0=MULT, op1=ADD, accum_out=sums[:, n : n + 1],
+            acc = ps_proj.tile([P, BLOCK], F32, name="acc")
+            for g in range(GROUPS):
+                nc.tensor.matmul_mx(
+                    out=acc[:],
+                    lhsT=aq[:, P * g : P * (g + 1)].bitcast(FP8X4),
+                    lhsT_scale=asc[:, P * g : P * (g + 1)],
+                    rhs=wp[:, g, 2 * BLOCK * n : 2 * BLOCK * (n + 1)].bitcast(FP4X4),
+                    rhs_scale=wp_sc[:, g, BLOCK * n : BLOCK * (n + 1)],
+                    start=(g == 0),
+                    stop=(g == GROUPS - 1),
                 )
-            state["xm", i] = xm
-            state["sums", i] = sums
-            nc.sync.dma_start(out=mid_hbm[:, i, :], in_=xm[:])
+            state["acc", i, n] = acc
+
+        def mid(i, n):
+            if ("mid", i) not in state:
+                state["mid", i] = work3.tile([P, D], F32, name="xm", align_bytes=64)
+                state["sums", i] = work3.tile([P, 2], F32, name="sums", align_bytes=64)
+            xm, sums = state["mid", i], state["sums", i]
+            cols = slice(BLOCK * n, BLOCK * (n + 1))
+            nc.vector.scalar_tensor_tensor(
+                out=xm[:, cols], in0=state["acc", i, n][:], scalar=1.0, in1=state["xb", i][:, cols],
+                op0=MULT, op1=ADD, accum_out=sums[:, n : n + 1],
+            )
+            nc.sync.dma_start(out=mid_hbm[:, i, cols], in_=xm[:, cols])
 
         def mean(i):
             sums = state["sums", i]
             nmu = work3.tile([P, 1], F32, name="nmu", align_bytes=64)
-            nc.gpsimd.tensor_scalar(out=nmu[:], in0=sums[:, 0:1], scalar1=sums[:, 1:2], scalar2=-1.0 / D, op0=ADD, op1=MULT)
-            state["xm", i] = (state["xm", i], nmu)
+            scrap = work3.tile([P, 2], F32, name="scrap", align_bytes=64)
+            nc.scalar.activation(out=scrap[:], in_=sums[:], func=COPY, scale=-1.0 / D, accum_out=nmu[:])
+            state["xm", i] = (state["mid", i], nmu)
 
         def spread(i):
-            if i == 0:
-                nc.gpsimd.tensor_copy(out=g_col[:], in_=g_raw[:])
-                nc.gpsimd.tensor_copy(out=b_col[:], in_=b_raw[:])
             xm, nmu = state["xm", i]
             junk = work.tile([P, D], BF16, name="junk", align_bytes=64)
             ssq = work3.tile([P, 1], F32, name="ssq", align_bytes=64)
             nc.scalar.activation(out=junk[:], in_=xm[:], func=SQUARE, bias=nmu[:], scale=1.0, accum_out=ssq[:])
             state["ssq", i] = ssq
 
+        def var(i):
+            v = work3.tile([P, 1], F32, name="v", align_bytes=64)
+            nc.gpsimd.tensor_scalar(out=v[:], in0=state["ssq", i][:], scalar1=1.0 / D, scalar2=EPS, op0=MULT, op1=ADD)
+            state["var", i] = v
+
         def rstd(i):
-            ssq = state["ssq", i]
-            var = work3.tile([P, 1], F32, name="var", align_bytes=64)
             rs = work3.tile([P, 1], F32, name="rs", align_bytes=64)
-            nc.gpsimd.tensor_scalar(out=var[:], in0=ssq[:], scalar1=1.0 / D, scalar2=EPS, op0=MULT, op1=ADD)
-            nc.gpsimd.tensor_tensor(out=rs[:], in0=var[:], in1=half[:], op=POW)
+            nc.gpsimd.tensor_tensor(out=rs[:], in0=state["var", i][:], in1=half[:], op=POW)
             state["rstd", i] = rs
 
         def norm(i):
@@ -274,7 +286,7 @@ def tile_flashinferblock_pb_w4_kernel(
             state["ht", i, g] = ht
 
         def weave(i, g):
-            if g == 0:
+            if ("hg", i) not in state:
                 state["hg", i] = work.tile([P, GROUPS, BLOCK], BF16, name="hg", align_bytes=64)
             state["woven", i, g] = True
             dst = state["hg", i][:, g, :].rearrange("p (c i t) -> p c t i", i=4, t=PACK)
@@ -311,7 +323,7 @@ def tile_flashinferblock_pb_w4_kernel(
             state["hacc", i, f] = acc
 
         def bias(i, f):
-            if f % 2 == 0:
+            if ("hid", i, f // 2) not in state:
                 state["hid", i, f // 2] = hids.tile([P, 2 * BLOCK], F32, name="hid", align_bytes=64)
             hid = state["hid", i, f // 2]
             o = BLOCK * (f % 2)
@@ -327,23 +339,52 @@ def tile_flashinferblock_pb_w4_kernel(
                 nc.scalar.activation(out=hid[:, w * c : w * (c + 1)], in_=hid[:, w * c : w * (c + 1)], func=GELU)
                 nc.sync.dma_start(out=hid_hbm[:, i, 2 * BLOCK * h + w * c : 2 * BLOCK * h + w * (c + 1)], in_=hid[:, w * c : w * (c + 1)])
 
-        stages = {
-            "widen": widen, "turn_attn": turn_attn, "lay_attn": lay_attn, "quant_attn": quant_attn, "pre_add": pre_add,
-            "project": project, "mid": mid, "mean": mean, "spread": spread, "rstd": rstd, "norm": norm,
-            "turn_norm0": lambda j: turn_norm(j, 0), "turn_norm1": lambda j: turn_norm(j, 1),
-            "gain0": lambda j: gain(j, 0), "gain1": lambda j: gain(j, 1),
-            "weave0": lambda j: weave(j, 0), "weave1": lambda j: weave(j, 1), "quant_norm": quant_norm,
-        }
-        events = []
-        for j in range(TILES):
-            for order, (name, (off, early)) in enumerate(OFF.items()):
-                events.append((8 * j + off - min(early * j, CAP), order + 100, stages[name], (j,)))
+        stages = {}
+        for name, stage in (
+            ("widen", widen), ("turn_attn", turn_attn), ("lay_attn", lay_attn), ("quant_attn", quant_attn),
+            ("mean", mean), ("spread", spread), ("var", var), ("rstd", rstd), ("norm", norm), ("quant_norm", quant_norm),
+        ):
+            stages[name] = stage
+        for name, stage, count in (
+            ("pre_add", pre_add, 2), ("project", project, 2), ("mid", mid, 2), ("turn_norm", turn_norm, 2), ("gain", gain, 2),
+            ("weave", weave, 2), ("expand", expand, 8), ("bias", bias, 8), ("act", act, 4),
+        ):
+            for n in range(count):
+                stages["%s%d" % (name, n)] = lambda i, stage=stage, n=n: stage(i, n)
+        def run(names, i):
+            for name in names.split():
+                if 0 <= i < TILES:
+                    stages[name](i)
+
+        nc.gpsimd.tensor_copy(out=g_col[:], in_=g_raw[:])
+        nc.gpsimd.tensor_copy(out=b_col[:], in_=b_raw[:])
+        ctx.enter_context(tc.manual_schedule())
+        for name, i in HEAD:
+            run(name, i)
+        for s in range(TILES):
+            run("norm turn_norm0 turn_norm1 gain0 gain1", s + 1)
+            for a in WIDE.get(s, ()):
+                run("widen turn_attn", a)
+            for a in FRONT.get(s, ()):
+                run("mid0 mid1 mean spread", a)
+            for a in WIDE.get(s, ()):
+                run("lay_attn", a)
+            for a in PRE.get(s, ()):
+                run("pre_add0 pre_add1", a)
+            for a in FRONT.get(s, ()):
+                run("var rstd", a)
             for f in range(8):
-                events.append((8 * j + f - AHEAD, 0, expand, (j, f)))
-                events.append((8 * j + f, 1, bias, (j, f)))
+                if f == WEAVE_AT:
+                    run("weave0", s + 1)
+                    for a in QUANT.get(s, ()):
+                        run("quant_attn project0 project1", a)
+                    run("weave1", s + 1)
+                if f == WEAVE_AT + 1:
+                    run("quant_norm", s + 1)
+                run("bias%d" % f, s)
+                if f + 2 < 8:
+                    run("expand%d" % (f + 2), s)
+                else:
+                    run("expand%d" % (f - 6), s + 1)
                 if f % 2 == 1:
-                    events.append((8 * j + f, 2, act, (j, f // 2)))
-        events.sort(key=lambda e: e[:2])
-        with tc.manual_schedule():
-            for e in events:
-                e[2](*e[3])
+                    run("act%d" % (f // 2), s)

@@ -14,7 +14,7 @@ EPS = 1e-5
 V_PRE = 3
 PROD_SG = ()
 WEAVE_G = ()
-WEAVE_S = ()
+WEAVE_S = (1, 2, 3)
 NORM_G = ()
 GAIN_V = ()
 LAY_V = ()
@@ -24,16 +24,17 @@ NAMES = (
     "gain0 weave0 gain1 weave1 quant_norm "
     "expand0 bias0 expand1 bias1 act0 expand2 bias2 expand3 bias3 act1 expand4 bias4 expand5 bias5 act2 expand6 bias6 expand7 bias7 act3"
 ).split(" ")
+WF_CUT = 4
 WEAVE_AT = 5
+PROJ_AT = 5
 HEAD = (
     ("widen turn_attn lay_attn", 0),
     ("widen turn_attn lay_attn", 1),
-    ("pre_add0", 0),
     ("quant_attn project0 project1", 0),
-    ("pre_add1", 0),
+    ("pre_add0 pre_add1", 0),
     ("mid0 mid1 mean spread", 0),
-    ("widen turn_attn lay_attn", 2),
     ("quant_attn project0 project1", 1),
+    ("widen turn_attn lay_attn", 2),
     ("var rstd", 0),
     ("pre_add0 pre_add1", 1),
     ("norm turn_norm0 turn_norm1 gain0 gain1", 0),
@@ -46,8 +47,8 @@ HEAD = (
     ("pre_add1", 2),
     ("quant_norm", 0),
     ("project0 project1", 2),
-    ("widen turn_attn lay_attn", 3),
     ("expand0 expand1", 0),
+    ("widen turn_attn lay_attn", 3),
 )
 FRONT = {0: (2,), 1: (3,), 2: (4,), 3: (5,), 4: (6,), 5: (7,)}
 QUANT = {0: (3,), 1: (4,), 2: (5,), 3: (6,), 4: (7,)}
@@ -100,7 +101,7 @@ def tile_flashinferblock_pb_w4_kernel(
         bf_all = keep.tile([P, F], BF16, name="bf_all", align_bytes=64)
         wp = keep.tile([P, GROUPS, 2 * D], U8, name="wp", align_bytes=64)
         wp_sc = keep.tile([P, GROUPS, D], U8, name="wp_sc", align_bytes=64)
-        wf = keep.tile([P, GROUPS, 2 * F], U8, name="wf", align_bytes=64)
+        wf = [keep.tile([P, GROUPS, 2 * F // WF_CUT], U8, name="wf%d" % c, align_bytes=64) for c in range(WF_CUT)]
         wf_sc = keep.tile([P, GROUPS, F], U8, name="wf_sc", align_bytes=64)
         g_raw = keep.tile([P, GROUPS, PACK], BF16, name="g_raw", align_bytes=64)
         b_raw = keep.tile([P, GROUPS, PACK], BF16, name="b_raw", align_bytes=64)
@@ -110,12 +111,11 @@ def tile_flashinferblock_pb_w4_kernel(
         half = keep.tile([P, 1], F32, name="half", align_bytes=64)
         warm = keep.tile([P, 1], F32, name="warm", align_bytes=64)
 
+        nc.vector.memset(warm[:], 0.0)
         nc.vector.memset(wp_sc[:].rearrange("p g n -> p (g n)").bitcast(I32), 0)
         nc.vector.memset(wf_sc[:].rearrange("p g n -> p (g n)").bitcast(I32), 0)
-        nc.vector.memset(warm[:], 0.0)
         nc.gpsimd.memset(half[:], -0.5)
         make_identity(nc, ident[:])
-        nc.scalar.activation(out=warm[:], in_=warm[:], func=GELU)
 
         def load_scales(tile, hbm):
             for q in range(4):
@@ -130,29 +130,37 @@ def tile_flashinferblock_pb_w4_kernel(
         def load_x(a, b):
             nc.sync.dma_start(out=x_all[:, a:b, :], in_=x_hbm[:, a:b, :])
 
-        def load_wf(a, b):
+        def load_wf(c):
+            w = 2 * F // WF_CUT
             nc.sync.dma_start(
-                out=wf[:, :, a:b].bitcast(I32),
-                in_=w_fc1_words[:, :, a:b].rearrange("g p b -> p g b").bitcast(I32),
+                out=wf[c][:].bitcast(I32),
+                in_=w_fc1_words[:, :, w * c : w * (c + 1)].rearrange("g p b -> p g b").bitcast(I32),
             )
 
-        nc.scalar.dma_start(out=scale_all[:], in_=attn_out_scale.rearrange("a b k -> (a b k)").partition_broadcast(P))
-        load_attn(0, 1)
-        load_attn(1, 2)
+        scale_row = attn_out_scale.rearrange("a b k -> (a b k)")
+        for h in range(2):
+            cols = slice(BLOCK * h, BLOCK * (h + 1))
+            nc.scalar.dma_start(out=scale_all[:, cols], in_=scale_row[cols].partition_broadcast(P))
+            load_attn(h, h + 1)
         load_scales(wp_sc, w_proj_scales)
         nc.sync.dma_start(out=wp[:], in_=w_proj_words.rearrange("g p b -> p g b"))
-        nc.scalar.dma_start(out=bp_all[:], in_=b_proj.partition_broadcast(P))
         load_x(0, 1)
+        nc.scalar.dma_start(out=bp_all[:], in_=b_proj.partition_broadcast(P))
         load_attn(2, 4)
         load_x(1, 3)
         for raw, vec in ((g_raw, g2), (b_raw, beta2)):
             nc.scalar.dma_start(out=raw[:], in_=vec.rearrange("(g p t) -> p g t", p=P, t=PACK))
+        nc.scalar.activation(out=warm[:], in_=warm[:], func=GELU)
         load_scales(wf_sc, w_fc1_scales)
-        load_wf(0, F)
-        nc.scalar.dma_start(out=bf_all[:], in_=b_fc1.partition_broadcast(P))
-        load_wf(F, 2 * F)
-        load_attn(4, 8)
-        load_x(3, 8)
+        load_wf(0)
+        for h in range(2):
+            cols = slice(F // 2 * h, F // 2 * (h + 1))
+            nc.scalar.dma_start(out=bf_all[:, cols], in_=b_fc1[cols].partition_broadcast(P))
+            load_wf(h + 1)
+            load_attn(4 + 2 * h, 6 + 2 * h)
+        load_x(3, 4)
+        load_wf(3)
+        load_x(4, 8)
 
         state = {}
 
@@ -166,7 +174,10 @@ def tile_flashinferblock_pb_w4_kernel(
                     nc.gpsimd.tensor_tensor(out=prod[:, cols], in0=wide[:, cols], in1=scale_all[:, cols], op=MULT)
                 state["prod", i] = prod
                 return
-            nc.vector.tensor_tensor(out=prod[:], in0=attn_codes[:, i, :].bitcast(F8), in1=scale_all[:], op=MULT)
+            parts = 2 if i == 0 else 1
+            for c in range(parts):
+                cols = slice(D // parts * c, D // parts * (c + 1))
+                nc.vector.tensor_tensor(out=prod[:, cols], in0=attn_codes[:, i, cols].bitcast(F8), in1=scale_all[:, cols], op=MULT)
             state["prod", i] = prod
 
         def turn_attn(i):
@@ -256,8 +267,8 @@ def tile_flashinferblock_pb_w4_kernel(
             xh = work.tile([P, D], F32, name="xh", align_bytes=64)
             eng = nc.gpsimd if i in NORM_G else nc.vector
             eng.tensor_scalar(
-                out=xh[:].rearrange("p (g t q) -> p g q t", g=GROUPS, t=PACK),
-                in0=xm[:].rearrange("p (g q t) -> p g q t", g=GROUPS, t=PACK),
+                out=xh[:].rearrange("p (u m e) -> p m u e", u=2, e=2),
+                in0=xm[:].rearrange("p (m u e) -> p m u e", u=2, e=2),
                 scalar1=nmu[:], scalar2=state["rstd", i][:], op0=ADD, op1=MULT,
             )
             state["xh", i] = xh
@@ -266,8 +277,8 @@ def tile_flashinferblock_pb_w4_kernel(
             xh = state["xh", i]
             turned = ps_turn.tile([P, PACK, P], F32, name="turned")
             for t in range(PACK):
-                j = PACK * g + t
-                nc.tensor.transpose(turned[:, t, :], xh[:, P * j : P * (j + 1)], ident[:])
+                first = D // 2 * (t // 2) + 2 * P * g + t % 2
+                nc.tensor.transpose(turned[:, t, :], xh[:, first : first + 2 * P - 1 : 2], ident[:])
             state["hturned", i, g] = turned
 
         def gain(i, g):
@@ -315,7 +326,7 @@ def tile_flashinferblock_pb_w4_kernel(
                     out=acc[:],
                     lhsT=hq[:, P * g : P * (g + 1)].bitcast(FP8X4),
                     lhsT_scale=hsc[:, P * g : P * (g + 1)],
-                    rhs=wf[:, g, 2 * BLOCK * f : 2 * BLOCK * (f + 1)].bitcast(FP4X4),
+                    rhs=wf[f // 2][:, g, 2 * BLOCK * (f % 2) : 2 * BLOCK * (f % 2 + 1)].bitcast(FP4X4),
                     rhs_scale=wf_sc[:, g, BLOCK * f : BLOCK * (f + 1)],
                     start=(g == 0),
                     stop=(g == GROUPS - 1),
@@ -327,17 +338,19 @@ def tile_flashinferblock_pb_w4_kernel(
                 state["hid", i, f // 2] = hids.tile([P, 2 * BLOCK], F32, name="hid", align_bytes=64)
             hid = state["hid", i, f // 2]
             o = BLOCK * (f % 2)
-            nc.vector.tensor_tensor(
-                out=hid[:, o : o + BLOCK], in0=state["hacc", i, f][:], in1=bf_all[:, BLOCK * f : BLOCK * (f + 1)], op=ADD
-            )
+            w = BLOCK // 2 if (i, f) == (TILES - 1, 7) else BLOCK
+            for c in range(0, BLOCK, w):
+                nc.vector.tensor_tensor(
+                    out=hid[:, o + c : o + c + w], in0=state["hacc", i, f][:, c : c + w],
+                    in1=bf_all[:, BLOCK * f + c : BLOCK * f + c + w], op=ADD,
+                )
 
         def act(i, h):
             hid = state["hid", i, h]
-            parts = 2 if (i == TILES - 1 and h == 3) else 1
-            w = 2 * BLOCK // parts
-            for c in range(parts):
-                nc.scalar.activation(out=hid[:, w * c : w * (c + 1)], in_=hid[:, w * c : w * (c + 1)], func=GELU)
-                nc.sync.dma_start(out=hid_hbm[:, i, 2 * BLOCK * h + w * c : 2 * BLOCK * h + w * (c + 1)], in_=hid[:, w * c : w * (c + 1)])
+            cuts = (0, 512, 768, 1024) if (i, h) == (TILES - 1, 3) else (0, 1024)
+            for a, b in zip(cuts[:-1], cuts[1:]):
+                nc.scalar.activation(out=hid[:, a:b], in_=hid[:, a:b], func=GELU)
+                nc.sync.dma_start(out=hid_hbm[:, i, 2 * BLOCK * h + a : 2 * BLOCK * h + b], in_=hid[:, a:b])
 
         stages = {}
         for name, stage in (
@@ -363,6 +376,8 @@ def tile_flashinferblock_pb_w4_kernel(
             run(name, i)
         for s in range(TILES):
             run("norm turn_norm0 turn_norm1 gain0 gain1", s + 1)
+            if s + 1 in WEAVE_S:
+                run("weave0 weave1", s + 1)
             for a in WIDE.get(s, ()):
                 run("widen turn_attn", a)
             for a in FRONT.get(s, ()):
@@ -375,10 +390,12 @@ def tile_flashinferblock_pb_w4_kernel(
                 run("var rstd", a)
             for f in range(8):
                 if f == WEAVE_AT:
-                    run("weave0", s + 1)
+                    if s + 1 not in WEAVE_S:
+                        run("weave0", s + 1)
                     for a in QUANT.get(s, ()):
-                        run("quant_attn project0 project1", a)
-                    run("weave1", s + 1)
+                        run("quant_attn", a)
+                    if s + 1 not in WEAVE_S:
+                        run("weave1", s + 1)
                 if f == WEAVE_AT + 1:
                     run("quant_norm", s + 1)
                 run("bias%d" % f, s)
@@ -386,5 +403,8 @@ def tile_flashinferblock_pb_w4_kernel(
                     run("expand%d" % (f + 2), s)
                 else:
                     run("expand%d" % (f - 6), s + 1)
+                if f == PROJ_AT:
+                    for a in QUANT.get(s, ()):
+                        run("project0 project1", a)
                 if f % 2 == 1:
                     run("act%d" % (f // 2), s)

@@ -14,7 +14,7 @@ EPS = 1e-5
 V_PRE = 3
 PROD_SG = ()
 WEAVE_G = ()
-WEAVE_S = (1, 2, 3)
+WEAVE_S = (2, 3, 4)
 NORM_G = ()
 GAIN_V = ()
 LAY_V = ()
@@ -25,30 +25,69 @@ NAMES = (
     "expand0 bias0 expand1 bias1 act0 expand2 bias2 expand3 bias3 act1 expand4 bias4 expand5 bias5 act2 expand6 bias6 expand7 bias7 act3"
 ).split(" ")
 WF_CUT = 4
+TURN_AT = 4
 WEAVE_AT = 5
 PROJ_AT = 5
+CAST_V = (0,)
+LATE = ()
 HEAD = (
-    ("widen turn_attn lay_attn", 0),
-    ("widen turn_attn lay_attn", 1),
-    ("quant_attn project0 project1", 0),
-    ("pre_add0 pre_add1", 0),
-    ("mid0 mid1 mean spread", 0),
-    ("quant_attn project0 project1", 1),
-    ("widen turn_attn lay_attn", 2),
-    ("var rstd", 0),
-    ("pre_add0 pre_add1", 1),
-    ("norm turn_norm0 turn_norm1 gain0 gain1", 0),
-    ("mid0 mid1 mean spread", 1),
-    ("var rstd", 1),
-    ("quant_attn", 2),
-    ("weave0", 0),
+    ("bias_tile", 4),
+    ("widen", 0),
+    ("widen", 1),
+    ("turn_attn", 0),
+    ("lay_attn", 0),
+    ("turn_attn", 1),
+    ("pre_add0", 0),
+    ("quant_attn", 0),
+    ("pre_add1", 0),
+    ("widen", 2),
+    ("lay_attn", 1),
+    ("project1", 0),
+    ("mid1", 0),
+    ("project0", 0),
+    ("mid0", 0),
+    ("mean", 0),
+    ("spread", 0),
+    ("var", 0),
+    ("turn_attn", 2),
+    ("quant_attn", 1),
+    ("rstd", 0),
+    ("pre_add0", 1),
+    ("widen", 4),
+    ("project0", 1),
+    ("pre_add1", 1),
+    ("project1", 1),
+    ("mid0", 1),
+    ("norm", 0),
+    ("widen", 3),
+    ("mid1", 1),
+    ("mean", 1),
+    ("turn_norm0", 0),
+    ("turn_norm1", 0),
+    ("gain0", 0),
+    ("gain1", 0),
+    ("spread", 1),
+    ("var", 1),
+    ("rstd", 1),
+    ("lay_attn", 2),
+    ("bias_tile", 1),
     ("pre_add0", 2),
-    ("weave1", 0),
     ("pre_add1", 2),
+    ("bias_tile", 2),
+    ("quant_attn", 2),
+    ("turn_attn", 3),
+    ("weave0", 0),
+    ("bias_tile", 0),
+    ("project1", 2),
+    ("bias_tile", 3),
+    ("project0", 2),
+    ("widen", 5),
+    ("weave1", 0),
     ("quant_norm", 0),
-    ("project0 project1", 2),
-    ("expand0 expand1", 0),
-    ("widen turn_attn lay_attn", 3),
+    ("expand0", 0),
+    ("widen", 7),
+    ("expand1", 0),
+    ("widen", 6),
 )
 FRONT = {0: (2,), 1: (3,), 2: (4,), 3: (5,), 4: (6,), 5: (7,)}
 QUANT = {0: (3,), 1: (4,), 2: (5,), 3: (6,), 4: (7,)}
@@ -95,7 +134,9 @@ def tile_flashinferblock_pb_w4_kernel(
         hid_hbm = out_1.flatten_outer_dims().rearrange("(p i) f -> p i f", i=TILES)
 
         attn_codes = keep.tile([P, TILES, D], U8, name="attn_codes", align_bytes=64)
-        scale_all = keep.tile([P, D], F32, name="scale_all", align_bytes=64)
+        s_col = keep.tile([P, GROUPS, PACK], F32, name="s_col", align_bytes=64)
+        rows = keep.tile([P, BLOCK], BF16, name="rows", align_bytes=64)
+        ident16 = keep.tile([P, P], BF16, name="ident16", align_bytes=64)
         x_all = keep.tile([P, TILES, D], BF16, name="x_all", align_bytes=64)
         bp_all = keep.tile([P, D], BF16, name="bp_all", align_bytes=64)
         bf_all = keep.tile([P, F], BF16, name="bf_all", align_bytes=64)
@@ -112,10 +153,12 @@ def tile_flashinferblock_pb_w4_kernel(
         warm = keep.tile([P, 1], F32, name="warm", align_bytes=64)
 
         nc.vector.memset(warm[:], 0.0)
+        nc.vector.memset(rows[:].bitcast(I32), 0)
         nc.vector.memset(wp_sc[:].rearrange("p g n -> p (g n)").bitcast(I32), 0)
         nc.vector.memset(wf_sc[:].rearrange("p g n -> p (g n)").bitcast(I32), 0)
         nc.gpsimd.memset(half[:], -0.5)
         make_identity(nc, ident[:])
+        make_identity(nc, ident16[:])
 
         def load_scales(tile, hbm):
             for q in range(4):
@@ -137,48 +180,47 @@ def tile_flashinferblock_pb_w4_kernel(
                 in_=w_fc1_words[:, :, w * c : w * (c + 1)].rearrange("g p b -> p g b").bitcast(I32),
             )
 
-        scale_row = attn_out_scale.rearrange("a b k -> (a b k)")
-        for h in range(2):
-            cols = slice(BLOCK * h, BLOCK * (h + 1))
-            nc.scalar.dma_start(out=scale_all[:, cols], in_=scale_row[cols].partition_broadcast(P))
-            load_attn(h, h + 1)
-        load_scales(wp_sc, w_proj_scales)
-        nc.sync.dma_start(out=wp[:], in_=w_proj_words.rearrange("g p b -> p g b"))
-        load_x(0, 1)
-        nc.scalar.dma_start(out=bp_all[:], in_=b_proj.partition_broadcast(P))
-        load_attn(2, 4)
-        load_x(1, 3)
+        load_attn(0, 1)
+        load_attn(1, 2)
+        nc.scalar.dma_start(out=s_col[:], in_=attn_out_scale.rearrange("a b (g p t) -> p (a b g) t", p=P, t=PACK))
+        nc.scalar.dma_start(out=rows[8:10, :], in_=b_proj.rearrange("(c n) -> c n", n=BLOCK))
+        nc.scalar.dma_start(out=rows[0:8, :], in_=b_fc1.rearrange("(c n) -> c n", n=BLOCK))
         for raw, vec in ((g_raw, g2), (b_raw, beta2)):
             nc.scalar.dma_start(out=raw[:], in_=vec.rearrange("(g p t) -> p g t", p=P, t=PACK))
         nc.scalar.activation(out=warm[:], in_=warm[:], func=GELU)
+        load_scales(wp_sc, w_proj_scales)
+        nc.sync.dma_start(out=wp[:], in_=w_proj_words.rearrange("g p b -> p g b"))
+        load_x(0, 1)
+        load_attn(2, 4)
+        load_x(1, 3)
         load_scales(wf_sc, w_fc1_scales)
+        load_attn(4, 6)
         load_wf(0)
-        for h in range(2):
-            cols = slice(F // 2 * h, F // 2 * (h + 1))
-            nc.scalar.dma_start(out=bf_all[:, cols], in_=b_fc1[cols].partition_broadcast(P))
-            load_wf(h + 1)
-            load_attn(4 + 2 * h, 6 + 2 * h)
+        load_wf(1)
+        load_attn(6, 8)
         load_x(3, 4)
+        load_wf(2)
         load_wf(3)
         load_x(4, 8)
 
         state = {}
 
+        def spread_bias(c):
+            acc = ps_hid.tile([P, 2, BLOCK], BF16, name="hacc")
+            for h in range(2):
+                r = 2 * c + h
+                nc.tensor.matmul(
+                    acc[:, h, :], lhsT=ident16[:, r : r + 1].to_broadcast([P, P]), rhs=rows[:], start=True, stop=True
+                )
+            state["biasdone", c] = True
+            dst = bp_all[:] if c == 4 else bf_all[:, 2 * BLOCK * c : 2 * BLOCK * (c + 1)]
+            nc.scalar.copy(out=dst, in_=acc[:].rearrange("p h n -> p (h n)"))
+
         def widen(i):
-            prod = keep.tile([P, D], BF16, name="prod%d" % i, align_bytes=64)
-            if i in PROD_SG:
-                wide = work.tile([P, D], BF16, name="wide", align_bytes=64)
-                nc.scalar.copy(out=wide[:], in_=attn_codes[:, i, :].bitcast(F8))
-                for c in range(G_CUT):
-                    cols = slice(D // G_CUT * c, D // G_CUT * (c + 1))
-                    nc.gpsimd.tensor_tensor(out=prod[:, cols], in0=wide[:, cols], in1=scale_all[:, cols], op=MULT)
-                state["prod", i] = prod
-                return
-            parts = 2 if i == 0 else 1
-            for c in range(parts):
-                cols = slice(D // parts * c, D // parts * (c + 1))
-                nc.vector.tensor_tensor(out=prod[:, cols], in0=attn_codes[:, i, cols].bitcast(F8), in1=scale_all[:, cols], op=MULT)
-            state["prod", i] = prod
+            wide = keep.tile([P, D], BF16, name="wide%d" % i, align_bytes=64)
+            cast = nc.vector.tensor_copy if i in CAST_V else nc.scalar.copy
+            cast(out=wide[:], in_=attn_codes[:, i, :].bitcast(F8))
+            state["prod", i] = wide
 
         def turn_attn(i):
             words = state["prod", i][:].bitcast(F32)
@@ -189,18 +231,21 @@ def tile_flashinferblock_pb_w4_kernel(
             state["turned", i] = turned
 
         def lay_attn(i):
-            ag = work.tile([P, D], BF16, name="ag", align_bytes=64)
-            lay_copy = nc.vector.tensor_copy if i in LAY_V else nc.scalar.copy
-            lay_copy(
-                out=ag[:].bitcast(F32).rearrange("p (g r u) -> p g r u", g=GROUPS, u=2),
-                in_=state["turned", i][:].rearrange("p g u r -> p g r u"),
-            )
+            ag = work.tile([P, GROUPS, BLOCK], BF16, name="ag", align_bytes=64)
+            for g in range(GROUPS):
+                words = state["turned", i][:, g].rearrange("p u r -> p (u r)").bitcast(BF16)
+                nc.vector.tensor_tensor(
+                    out=ag[:, g, :].rearrange("p (r u e) -> p r u e", u=2, e=2),
+                    in0=words.rearrange("p (u r e) -> p r u e", u=2, e=2),
+                    in1=s_col[:, g, :].rearrange("p (o u e) -> p o u e", o=1, u=2).to_broadcast([P, P, 2, 2]),
+                    op=MULT,
+                )
             state["ag", i] = ag
 
         def quant_attn(i):
             aq = work3.tile([P, GROUPS * P], U32, name="aq", align_bytes=64)
             asc = work3.tile([P, GROUPS * P], U8, name="asc", align_bytes=64)
-            nc.vector.quantize_mx(out=aq[:].bitcast(FP8X4), scales=asc[:], in_=state["ag", i][:])
+            nc.vector.quantize_mx(out=aq[:].bitcast(FP8X4), scales=asc[:], in_=state["ag", i][:].rearrange("p g c -> p (g c)"))
             state["aq", i] = (aq, asc)
 
         def pre_add(i, c):
@@ -209,6 +254,7 @@ def tile_flashinferblock_pb_w4_kernel(
             xb = state["xb", i]
             eng = nc.vector if i < V_PRE else nc.gpsimd
             cols = slice(BLOCK * c, BLOCK * (c + 1))
+            state["xbdone", i, c] = state["biasdone", 4]
             eng.tensor_tensor(out=xb[:, cols], in0=x_all[:, i, cols], in1=bp_all[:, cols], op=ADD)
 
         def project(i, n):
@@ -232,6 +278,8 @@ def tile_flashinferblock_pb_w4_kernel(
                 state["sums", i] = work3.tile([P, 2], F32, name="sums", align_bytes=64)
             xm, sums = state["mid", i], state["sums", i]
             cols = slice(BLOCK * n, BLOCK * (n + 1))
+            assert state["xbdone", i, n]
+            state["middone", i, n] = True
             nc.vector.scalar_tensor_tensor(
                 out=xm[:, cols], in0=state["acc", i, n][:], scalar=1.0, in1=state["xb", i][:, cols],
                 op0=MULT, op1=ADD, accum_out=sums[:, n : n + 1],
@@ -240,6 +288,7 @@ def tile_flashinferblock_pb_w4_kernel(
 
         def mean(i):
             sums = state["sums", i]
+            assert state["middone", i, 0] and state["middone", i, 1]
             nmu = work3.tile([P, 1], F32, name="nmu", align_bytes=64)
             scrap = work3.tile([P, 2], F32, name="scrap", align_bytes=64)
             nc.scalar.activation(out=scrap[:], in_=sums[:], func=COPY, scale=-1.0 / D, accum_out=nmu[:])
@@ -334,6 +383,7 @@ def tile_flashinferblock_pb_w4_kernel(
             state["hacc", i, f] = acc
 
         def bias(i, f):
+            assert state["biasdone", f // 2]
             if ("hid", i, f // 2) not in state:
                 state["hid", i, f // 2] = hids.tile([P, 2 * BLOCK], F32, name="hid", align_bytes=64)
             hid = state["hid", i, f // 2]
@@ -347,7 +397,7 @@ def tile_flashinferblock_pb_w4_kernel(
 
         def act(i, h):
             hid = state["hid", i, h]
-            cuts = (0, 512, 768, 1024) if (i, h) == (TILES - 1, 3) else (0, 1024)
+            cuts = (0, 1024) if i < TILES - 1 else (0, 512, 1024) if h < 3 else (0, 512, 768, 1024)
             for a, b in zip(cuts[:-1], cuts[1:]):
                 nc.scalar.activation(out=hid[:, a:b], in_=hid[:, a:b], func=GELU)
                 nc.sync.dma_start(out=hid_hbm[:, i, 2 * BLOCK * h + a : 2 * BLOCK * h + b], in_=hid[:, a:b])
@@ -373,17 +423,18 @@ def tile_flashinferblock_pb_w4_kernel(
         nc.gpsimd.tensor_copy(out=b_col[:], in_=b_raw[:])
         ctx.enter_context(tc.manual_schedule())
         for name, i in HEAD:
-            run(name, i)
+            if name == "bias_tile":
+                spread_bias(i)
+            else:
+                run(name, i)
         for s in range(TILES):
             run("norm turn_norm0 turn_norm1 gain0 gain1", s + 1)
             if s + 1 in WEAVE_S:
                 run("weave0 weave1", s + 1)
-            for a in WIDE.get(s, ()):
-                run("widen turn_attn", a)
+            for a in QUANT.get(s, ()):
+                run("lay_attn", a)
             for a in FRONT.get(s, ()):
                 run("mid0 mid1 mean spread", a)
-            for a in WIDE.get(s, ()):
-                run("lay_attn", a)
             for a in PRE.get(s, ()):
                 run("pre_add0 pre_add1", a)
             for a in FRONT.get(s, ()):
@@ -403,6 +454,9 @@ def tile_flashinferblock_pb_w4_kernel(
                     run("expand%d" % (f + 2), s)
                 else:
                     run("expand%d" % (f - 6), s + 1)
+                if f == TURN_AT:
+                    for a in WIDE.get(s, ()):
+                        run(("widen " if a in LATE else "") + "turn_attn", a)
                 if f == PROJ_AT:
                     for a in QUANT.get(s, ()):
                         run("project0 project1", a)

from contextlib import ExitStack

import concourse.mybir as mybir
from concourse.masks import make_identity

P = 128
TILES = 8
D = 1024
F = 4096
GROUPS = 2
PACK = 4
BLOCK = 512
EPS = 1e-5
V_PRE = 3
PROD_SG = ()
WEAVE_G = ()
WEAVE_S = (2, 3, 4)
NORM_G = ()
GAIN_V = ()
LAY_V = ()
G_CUT = 2
NAMES = (
    "widen turn_attn lay_attn quant_attn pre_add0 pre_add1 project0 project1 mid0 mid1 mean spread rstd norm turn_norm0 turn_norm1 "
    "gain0 weave0 gain1 weave1 quant_norm "
    "expand0 bias0 expand1 bias1 act0 expand2 bias2 expand3 bias3 act1 expand4 bias4 expand5 bias5 act2 expand6 bias6 expand7 bias7 act3"
).split(" ")
WF_CUT = 4
TURN_AT = 4
WEAVE_AT = 5
PROJ_AT = 5
CAST_V = (0,)
LATE = ()
HEAD = (
    ("bias_tile", 4),
    ("widen", 0),
    ("widen", 1),
    ("turn_attn", 0),
    ("lay_attn", 0),
    ("turn_attn", 1),
    ("pre_add0", 0),
    ("quant_attn", 0),
    ("pre_add1", 0),
    ("widen", 2),
    ("lay_attn", 1),
    ("project1", 0),
    ("mid1", 0),
    ("project0", 0),
    ("mid0", 0),
    ("mean", 0),
    ("spread", 0),
    ("var", 0),
    ("turn_attn", 2),
    ("quant_attn", 1),
    ("rstd", 0),
    ("pre_add0", 1),
    ("widen", 4),
    ("project0", 1),
    ("pre_add1", 1),
    ("project1", 1),
    ("mid0", 1),
    ("norm", 0),
    ("widen", 3),
    ("mid1", 1),
    ("mean", 1),
    ("turn_norm0", 0),
    ("turn_norm1", 0),
    ("gain0", 0),
    ("gain1", 0),
    ("spread", 1),
    ("var", 1),
    ("rstd", 1),
    ("lay_attn", 2),
    ("bias_tile", 1),
    ("pre_add0", 2),
    ("pre_add1", 2),
    ("bias_tile", 2),
    ("quant_attn", 2),
    ("turn_attn", 3),
    ("weave0", 0),
    ("bias_tile", 0),
    ("project1", 2),
    ("bias_tile", 3),
    ("project0", 2),
    ("widen", 5),
    ("weave1", 0),
    ("quant_norm", 0),
    ("expand0", 0),
    ("widen", 7),
    ("expand1", 0),
    ("widen", 6),
)
FRONT = {0: (2,), 1: (3,), 2: (4,), 3: (5,), 4: (6,), 5: (7,)}
QUANT = {0: (3,), 1: (4,), 2: (5,), 3: (6,), 4: (7,)}
WIDE = {0: (4,), 1: (5,), 2: (6,), 3: (7,)}
PRE = {0: (3,), 1: (4,), 2: (5,), 3: (6,), 4: (7,)}

FLOPS = 2 * TILES * P * D * (D + F)

F32 = mybir.dt.float32
BF16 = mybir.dt.bfloat16
I32 = mybir.dt.int32
U32 = mybir.dt.uint32
U8 = mybir.dt.uint8
F8 = mybir.dt.float8_e4m3fn
FP8X4 = mybir.dt.float8_e4m3fn_x4
FP4X4 = mybir.dt.float4_e2m1fn_x4

ADD = mybir.AluOpType.add
MULT = mybir.AluOpType.mult
POW = mybir.AluOpType.pow
IDENTITY = mybir.ActivationFunctionType.Identity
COPY = mybir.ActivationFunctionType.Copy
SQUARE = mybir.ActivationFunctionType.Square
GELU = mybir.ActivationFunctionType.Gelu


def tile_flashinferblock_pb_w4_kernel(
    tc, attn_out_bytes, attn_out_scale, x, w_proj_words, w_proj_scales, b_proj, g2, beta2,
    w_fc1_words, w_fc1_scales, b_fc1, out_0, out_1,
):
    nc = tc.nc
    with ExitStack() as ctx:
        keep = ctx.enter_context(tc.tile_pool(name="keep", bufs=1))
        work = ctx.enter_context(tc.tile_pool(name="work", bufs=2))
        work3 = ctx.enter_context(tc.tile_pool(name="work3", bufs=4))
        hids = ctx.enter_context(tc.tile_pool(name="hids", bufs=8))
        ps_turn = ctx.enter_context(tc.psum_pool(name="ps_turn", bufs=3))
        ps_proj = ctx.enter_context(tc.psum_pool(name="ps_proj", bufs=2))
        ps_hid = ctx.enter_context(tc.psum_pool(name="ps_hid", bufs=3))

        attn_hbm = attn_out_bytes.flatten_outer_dims().rearrange("(p i) d -> p i d", i=TILES)
        x_hbm = x.flatten_outer_dims().rearrange("(p i) d -> p i d", i=TILES)
        mid_hbm = out_0.flatten_outer_dims().rearrange("(p i) d -> p i d", i=TILES)
        hid_hbm = out_1.flatten_outer_dims().rearrange("(p i) f -> p i f", i=TILES)

        attn_codes = keep.tile([P, TILES, D], U8, name="attn_codes", align_bytes=64)
        s_col = keep.tile([P, GROUPS, PACK], F32, name="s_col", align_bytes=64)
        rows = keep.tile([P, BLOCK], BF16, name="rows", align_bytes=64)
        ident16 = keep.tile([P, P], BF16, name="ident16", align_bytes=64)
        x_all = keep.tile([P, TILES, D], BF16, name="x_all", align_bytes=64)
        bp_all = keep.tile([P, D], BF16, name="bp_all", align_bytes=64)
        bf_all = keep.tile([P, F], BF16, name="bf_all", align_bytes=64)
        wp = keep.tile([P, GROUPS, 2 * D], U8, name="wp", align_bytes=64)
        wp_sc = keep.tile([P, GROUPS, D], U8, name="wp_sc", align_bytes=64)
        wf = [keep.tile([P, GROUPS, 2 * F // WF_CUT], U8, name="wf%d" % c, align_bytes=64) for c in range(WF_CUT)]
        wf_sc = keep.tile([P, GROUPS, F], U8, name="wf_sc", align_bytes=64)
        g_raw = keep.tile([P, GROUPS, PACK], BF16, name="g_raw", align_bytes=64)
        b_raw = keep.tile([P, GROUPS, PACK], BF16, name="b_raw", align_bytes=64)
        g_col = keep.tile([P, GROUPS, PACK], F32, name="g_col", align_bytes=64)
        b_col = keep.tile([P, GROUPS, PACK], F32, name="b_col", align_bytes=64)
        ident = keep.tile([P, P], F32, name="ident", align_bytes=64)
        half = keep.tile([P, 1], F32, name="half", align_bytes=64)
        warm = keep.tile([P, 1], F32, name="warm", align_bytes=64)

        nc.vector.memset(warm[:], 0.0)
        nc.vector.memset(rows[:].bitcast(I32), 0)
        nc.vector.memset(wp_sc[:].rearrange("p g n -> p (g n)").bitcast(I32), 0)
        nc.vector.memset(wf_sc[:].rearrange("p g n -> p (g n)").bitcast(I32), 0)
        nc.gpsimd.memset(half[:], -0.5)
        make_identity(nc, ident[:])
        make_identity(nc, ident16[:])

        def load_scales(tile, hbm):
            for q in range(4):
                nc.sync.dma_start(
                    out=tile[32 * q : 32 * q + 4, :, :].bitcast(I32),
                    in_=hbm[:, 4 * q : 4 * q + 4, :].rearrange("g q n -> q g n").bitcast(I32),
                )

        def load_attn(a, b):
            nc.sync.dma_start(out=attn_codes[:, a:b, :], in_=attn_hbm[:, a:b, :])

        def load_x(a, b):
            nc.sync.dma_start(out=x_all[:, a:b, :], in_=x_hbm[:, a:b, :])

        def load_wf(c):
            w = 2 * F // WF_CUT
            nc.sync.dma_start(
                out=wf[c][:].bitcast(I32),
                in_=w_fc1_words[:, :, w * c : w * (c + 1)].rearrange("g p b -> p g b").bitcast(I32),
            )

        load_attn(0, 1)
        load_attn(1, 2)
        nc.scalar.dma_start(out=s_col[:], in_=attn_out_scale.rearrange("a b (g p t) -> p (a b g) t", p=P, t=PACK))
        nc.scalar.dma_start(out=rows[8:10, :], in_=b_proj.rearrange("(c n) -> c n", n=BLOCK))
        nc.scalar.dma_start(out=rows[0:8, :], in_=b_fc1.rearrange("(c n) -> c n", n=BLOCK))
        for raw, vec in ((g_raw, g2), (b_raw, beta2)):
            nc.scalar.dma_start(out=raw[:], in_=vec.rearrange("(g p t) -> p g t", p=P, t=PACK))
        nc.scalar.activation(out=warm[:], in_=warm[:], func=GELU)
        load_scales(wp_sc, w_proj_scales)
        nc.sync.dma_start(out=wp[:], in_=w_proj_words.rearrange("g p b -> p g b"))
        load_x(0, 1)
        load_attn(2, 4)
        load_x(1, 3)
        load_scales(wf_sc, w_fc1_scales)
        load_attn(4, 6)
        load_wf(0)
        load_wf(1)
        load_attn(6, 8)
        load_x(3, 4)
        load_wf(2)
        load_wf(3)
        load_x(4, 8)

        state = {}

        def spread_bias(c):
            acc = ps_hid.tile([P, 2, BLOCK], BF16, name="hacc")
            for h in range(2):
                r = 2 * c + h
                nc.tensor.matmul(
                    acc[:, h, :], lhsT=ident16[:, r : r + 1].to_broadcast([P, P]), rhs=rows[:], start=True, stop=True
                )
            state["biasdone", c] = True
            dst = bp_all[:] if c == 4 else bf_all[:, 2 * BLOCK * c : 2 * BLOCK * (c + 1)]
            nc.scalar.copy(out=dst, in_=acc[:].rearrange("p h n -> p (h n)"))

        def widen(i):
            wide = keep.tile([P, D], BF16, name="wide%d" % i, align_bytes=64)
            cast = nc.vector.tensor_copy if i in CAST_V else nc.scalar.copy
            cast(out=wide[:], in_=attn_codes[:, i, :].bitcast(F8))
            state["prod", i] = wide

        def turn_attn(i):
            words = state["prod", i][:].bitcast(F32)
            turned = ps_turn.tile([P, GROUPS, 2, P], F32, name="turned")
            for g in range(GROUPS):
                for u in range(2):
                    nc.tensor.transpose(turned[:, g, u, :], words[:, 256 * g + u : 256 * (g + 1) : 2], ident[:])
            state["turned", i] = turned

        def lay_attn(i):
            ag = work.tile([P, GROUPS, BLOCK], BF16, name="ag", align_bytes=64)
            for g in range(GROUPS):
                words = state["turned", i][:, g].rearrange("p u r -> p (u r)").bitcast(BF16)
                nc.vector.tensor_tensor(
                    out=ag[:, g, :].rearrange("p (r u e) -> p r u e", u=2, e=2),
                    in0=words.rearrange("p (u r e) -> p r u e", u=2, e=2),
                    in1=s_col[:, g, :].rearrange("p (o u e) -> p o u e", o=1, u=2).to_broadcast([P, P, 2, 2]),
                    op=MULT,
                )
            state["ag", i] = ag

        def quant_attn(i):
            aq = work3.tile([P, GROUPS * P], U32, name="aq", align_bytes=64)
            asc = work3.tile([P, GROUPS * P], U8, name="asc", align_bytes=64)
            nc.vector.quantize_mx(out=aq[:].bitcast(FP8X4), scales=asc[:], in_=state["ag", i][:].rearrange("p g c -> p (g c)"))
            state["aq", i] = (aq, asc)

        def pre_add(i, c):
            if ("xb", i) not in state:
                state["xb", i] = work3.tile([P, D], F32, name="xb", align_bytes=64)
            xb = state["xb", i]
            eng = nc.vector if i < V_PRE else nc.gpsimd
            cols = slice(BLOCK * c, BLOCK * (c + 1))
            state["xbdone", i, c] = state["biasdone", 4]
            eng.tensor_tensor(out=xb[:, cols], in0=x_all[:, i, cols], in1=bp_all[:, cols], op=ADD)

        def project(i, n):
            aq, asc = state["aq", i]
            acc = ps_proj.tile([P, BLOCK], F32, name="acc")
            for g in range(GROUPS):
                nc.tensor.matmul_mx(
                    out=acc[:],
                    lhsT=aq[:, P * g : P * (g + 1)].bitcast(FP8X4),
                    lhsT_scale=asc[:, P * g : P * (g + 1)],
                    rhs=wp[:, g, 2 * BLOCK * n : 2 * BLOCK * (n + 1)].bitcast(FP4X4),
                    rhs_scale=wp_sc[:, g, BLOCK * n : BLOCK * (n + 1)],
                    start=(g == 0),
                    stop=(g == GROUPS - 1),
                )
            state["acc", i, n] = acc

        def mid(i, n):
            if ("mid", i) not in state:
                state["mid", i] = work3.tile([P, D], F32, name="xm", align_bytes=64)
                state["sums", i] = work3.tile([P, 2], F32, name="sums", align_bytes=64)
            xm, sums = state["mid", i], state["sums", i]
            cols = slice(BLOCK * n, BLOCK * (n + 1))
            assert state["xbdone", i, n]
            state["middone", i, n] = True
            nc.vector.scalar_tensor_tensor(
                out=xm[:, cols], in0=state["acc", i, n][:], scalar=1.0, in1=state["xb", i][:, cols],
                op0=MULT, op1=ADD, accum_out=sums[:, n : n + 1],
            )
            nc.sync.dma_start(out=mid_hbm[:, i, cols], in_=xm[:, cols])

        def mean(i):
            sums = state["sums", i]
            assert state["middone", i, 0] and state["middone", i, 1]
            nmu = work3.tile([P, 1], F32, name="nmu", align_bytes=64)
            scrap = work3.tile([P, 2], F32, name="scrap", align_bytes=64)
            nc.scalar.activation(out=scrap[:], in_=sums[:], func=COPY, scale=-1.0 / D, accum_out=nmu[:])
            state["xm", i] = (state["mid", i], nmu)

        def spread(i):
            xm, nmu = state["xm", i]
            junk = work.tile([P, D], BF16, name="junk", align_bytes=64)
            ssq = work3.tile([P, 1], F32, name="ssq", align_bytes=64)
            nc.scalar.activation(out=junk[:], in_=xm[:], func=SQUARE, bias=nmu[:], scale=1.0, accum_out=ssq[:])
            state["ssq", i] = ssq

        def var(i):
            v = work3.tile([P, 1], F32, name="v", align_bytes=64)
            nc.gpsimd.tensor_scalar(out=v[:], in0=state["ssq", i][:], scalar1=1.0 / D, scalar2=EPS, op0=MULT, op1=ADD)
            state["var", i] = v

        def rstd(i):
            rs = work3.tile([P, 1], F32, name="rs", align_bytes=64)
            nc.gpsimd.tensor_tensor(out=rs[:], in0=state["var", i][:], in1=half[:], op=POW)
            state["rstd", i] = rs

        def norm(i):
            xm, nmu = state["xm", i]
            xh = work.tile([P, D], F32, name="xh", align_bytes=64)
            eng = nc.gpsimd if i in NORM_G else nc.vector
            eng.tensor_scalar(
                out=xh[:].rearrange("p (u m e) -> p m u e", u=2, e=2),
                in0=xm[:].rearrange("p (m u e) -> p m u e", u=2, e=2),
                scalar1=nmu[:], scalar2=state["rstd", i][:], op0=ADD, op1=MULT,
            )
            state["xh", i] = xh

        def turn_norm(i, g):
            xh = state["xh", i]
            turned = ps_turn.tile([P, PACK, P], F32, name="turned")
            for t in range(PACK):
                first = D // 2 * (t // 2) + 2 * P * g + t % 2
                nc.tensor.transpose(turned[:, t, :], xh[:, first : first + 2 * P - 1 : 2], ident[:])
            state["hturned", i, g] = turned

        def gain(i, g):
            ht = work3.tile([P, PACK, P], BF16, name="ht", align_bytes=64)
            for t in range(PACK):
                if (i, g) in GAIN_V:
                    nc.vector.tensor_scalar(
                        out=ht[:, t, :], in0=state["hturned", i, g][:, t, :],
                        scalar1=g_col[:, g, t : t + 1], scalar2=b_col[:, g, t : t + 1], op0=MULT, op1=ADD,
                    )
                    continue
                nc.scalar.activation(
                    out=ht[:, t, :], in_=state["hturned", i, g][:, t, :], func=IDENTITY,
                    bias=b_col[:, g, t : t + 1], scale=g_col[:, g, t : t + 1],
                )
            state["ht", i, g] = ht

        def weave(i, g):
            if ("hg", i) not in state:
                state["hg", i] = work.tile([P, GROUPS, BLOCK], BF16, name="hg", align_bytes=64)
            state["woven", i, g] = True
            dst = state["hg", i][:, g, :].rearrange("p (c i t) -> p c t i", i=4, t=PACK)
            src = state["ht", i, g][:].rearrange("p t (c i) -> p c t i", i=4)
            if i in WEAVE_G:
                nc.gpsimd.tensor_scalar(out=dst, in0=src, scalar1=1.0, scalar2=0.0, op0=MULT, op1=ADD)
            elif i in WEAVE_S:
                nc.scalar.copy(out=dst, in_=src)
            else:
                nc.vector.tensor_copy(out=dst, in_=src)

        def quant_norm(i):
            assert state["woven", i, 0] and state["woven", i, 1]
            hq = work.tile([P, GROUPS * P], U32, name="hq", align_bytes=64)
            hsc = work.tile([P, GROUPS * P], U8, name="hsc", align_bytes=64)
            nc.vector.quantize_mx(
                out=hq[:].bitcast(FP8X4), scales=hsc[:], in_=state["hg", i][:].rearrange("p g c -> p (g c)")
            )
            state["hq", i] = (hq, hsc)

        def expand(i, f):
            hq, hsc = state["hq", i]
            acc = ps_hid.tile([P, BLOCK], F32, name="hacc")
            for g in range(GROUPS):
                nc.tensor.matmul_mx(
                    out=acc[:],
                    lhsT=hq[:, P * g : P * (g + 1)].bitcast(FP8X4),
                    lhsT_scale=hsc[:, P * g : P * (g + 1)],
                    rhs=wf[f // 2][:, g, 2 * BLOCK * (f % 2) : 2 * BLOCK * (f % 2 + 1)].bitcast(FP4X4),
                    rhs_scale=wf_sc[:, g, BLOCK * f : BLOCK * (f + 1)],
                    start=(g == 0),
                    stop=(g == GROUPS - 1),
                )
            state["hacc", i, f] = acc

        def bias(i, f):
            assert state["biasdone", f // 2]
            if ("hid", i, f // 2) not in state:
                state["hid", i, f // 2] = hids.tile([P, 2 * BLOCK], F32, name="hid", align_bytes=64)
            hid = state["hid", i, f // 2]
            o = BLOCK * (f % 2)
            w = BLOCK // 2 if (i, f) == (TILES - 1, 7) else BLOCK
            for c in range(0, BLOCK, w):
                nc.vector.tensor_tensor(
                    out=hid[:, o + c : o + c + w], in0=state["hacc", i, f][:, c : c + w],
                    in1=bf_all[:, BLOCK * f + c : BLOCK * f + c + w], op=ADD,
                )

        def act(i, h):
            hid = state["hid", i, h]
            cuts = (0, 1024) if i < TILES - 1 else (0, 512, 1024) if h < 3 else (0, 512, 768, 1024)
            for a, b in zip(cuts[:-1], cuts[1:]):
                nc.scalar.activation(out=hid[:, a:b], in_=hid[:, a:b], func=GELU)
                nc.sync.dma_start(out=hid_hbm[:, i, 2 * BLOCK * h + a : 2 * BLOCK * h + b], in_=hid[:, a:b])

        stages = {}
        for name, stage in (
            ("widen", widen), ("turn_attn", turn_attn), ("lay_attn", lay_attn), ("quant_attn", quant_attn),
            ("mean", mean), ("spread", spread), ("var", var), ("rstd", rstd), ("norm", norm), ("quant_norm", quant_norm),
        ):
            stages[name] = stage
        for name, stage, count in (
            ("pre_add", pre_add, 2), ("project", project, 2), ("mid", mid, 2), ("turn_norm", turn_norm, 2), ("gain", gain, 2),
            ("weave", weave, 2), ("expand", expand, 8), ("bias", bias, 8), ("act", act, 4),
        ):
            for n in range(count):
                stages["%s%d" % (name, n)] = lambda i, stage=stage, n=n: stage(i, n)
        def run(names, i):
            for name in names.split():
                if 0 <= i < TILES:
                    stages[name](i)

        nc.gpsimd.tensor_copy(out=g_col[:], in_=g_raw[:])
        nc.gpsimd.tensor_copy(out=b_col[:], in_=b_raw[:])
        ctx.enter_context(tc.manual_schedule())
        for name, i in HEAD:
            if name == "bias_tile":
                spread_bias(i)
            else:
                run(name, i)
        for s in range(TILES):
            run("norm turn_norm0 turn_norm1 gain0 gain1", s + 1)
            if s + 1 in WEAVE_S:
                run("weave0 weave1", s + 1)
            for a in QUANT.get(s, ()):
                run("lay_attn", a)
            for a in FRONT.get(s, ()):
                run("mid0 mid1 mean spread", a)
            for a in PRE.get(s, ()):
                run("pre_add0 pre_add1", a)
            for a in FRONT.get(s, ()):
                run("var rstd", a)
            for f in range(8):
                if f == WEAVE_AT:
                    if s + 1 not in WEAVE_S:
                        run("weave0", s + 1)
                    for a in QUANT.get(s, ()):
                        run("quant_attn", a)
                    if s + 1 not in WEAVE_S:
                        run("weave1", s + 1)
                if f == WEAVE_AT + 1:
                    run("quant_norm", s + 1)
                run("bias%d" % f, s)
                if f + 2 < 8:
                    run("expand%d" % (f + 2), s)
                else:
                    run("expand%d" % (f - 6), s + 1)
                if f == TURN_AT:
                    for a in WIDE.get(s, ()):
                        run(("widen " if a in LATE else "") + "turn_attn", a)
                if f == PROJ_AT:
                    for a in QUANT.get(s, ()):
                        run("project0 project1", a)
                if f % 2 == 1:
                    run("act%d" % (f // 2), s)
